import numpy as np
import ml_dtypes


def mxq(x, axis, fmt="e4m3"):
    dtype, down = {"e4m3": (ml_dtypes.float8_e4m3fn, 7), "e5m2": (ml_dtypes.float8_e5m2, 14)}[fmt]
    v = np.moveaxis(np.asarray(x, np.float32).astype(ml_dtypes.bfloat16).astype(np.float64), axis, -1)
    blocks = v.reshape(v.shape[:-1] + (-1, 32))
    amax = np.abs(blocks).max(-1, keepdims=True)
    byte = np.maximum(np.where(amax > 0, np.frexp(amax)[1] - 1 + 127, 0) - down, 1)
    scale = np.exp2(byte - 127.0)
    codes = (blocks / scale).astype(np.float32).astype(dtype).astype(np.float64)
    return np.moveaxis((codes * scale).reshape(v.shape), -1, axis)


WIDE = False


def mx_kscale(k):
    if not WIDE:
        return np.ones(k)
    levels = np.array([10, -10, 5, -5, 0])
    if k % 512:
        return np.exp2(np.random.permutation(np.resize(levels, k // 32))).repeat(32)
    a = np.empty((k // 512, 16))
    for p in range(k // 512):
        a[p, :8] = np.random.permutation(np.resize(levels, 8))
        for g in range(8):
            far = levels[np.abs(levels - a[p, g]) >= 10]
            a[p, g + 8] = far[np.random.randint(len(far))]
    return np.exp2(a.ravel()).repeat(32)


BF16 = ml_dtypes.bfloat16


def bf(x):
    return np.asarray(x, np.float32).astype(BF16)


def f64(x):
    return np.asarray(x).astype(np.float64)


B, OBS, ACT, U, KSUB = 1024, 383, 128, 1024, 2
DT = 1.0 / KSUB
LN_EPS = 1e-5


def mish(v):
    return v * np.tanh(np.log(1.0 + np.exp(v)))


def layer_norm(v, g, b):
    mu = v.mean(-1, keepdims=True)
    var = np.square(v - mu).mean(-1, keepdims=True)
    return (v - mu) / np.sqrt(var + LN_EPS) * g + b


def setup_inputs():
    s, t = mx_kscale(U), mx_kscale(U)
    return {"h0": bf(np.random.standard_normal((B, U)) * s),
            "z": bf(np.random.standard_normal((B, ACT)) * 0.5),
            "k1": bf(np.random.standard_normal((B, ACT))),
            "W1": bf(np.random.standard_normal((U, U)) / np.sqrt(U) / s[:, None]),
            "b1": bf(np.random.standard_normal(U) * 0.3),
            "ln1_g": bf((1.0 + 0.1 * np.random.standard_normal(U)) * t),
            "ln1_b": bf(0.1 * np.random.standard_normal(U) * t),
            "W2": bf(np.random.standard_normal((U, ACT)) / np.sqrt(U) / t[:, None]),
            "b2": bf(np.random.standard_normal(ACT) * 0.3)}


def reference(h0, z, k1, W1, b1, ln1_g, ln1_b, W2, b2):
    h1 = layer_norm(mish((mxq(f64(h0), 1, "e4m3") @ mxq(f64(W1), 0, "e4m3")) + f64(b1)), f64(ln1_g), f64(ln1_b))
    k2 = (mxq(h1, 1, "e4m3") @ mxq(f64(W2), 0, "e4m3")) + f64(b2)
    return f64(z) + (DT / 2.0) * (f64(k1) + k2)

@@ -1,0 +1,447 @@
+from contextlib import ExitStack
+
+import concourse.mybir as mybir
+from concourse.masks import make_identity
+
+F32 = mybir.dt.float32
+BF16 = mybir.dt.bfloat16
+U32 = mybir.dt.uint32
+U8 = mybir.dt.uint8
+FP8X4 = mybir.dt.float8_e4m3fn_x4
+FUNC = mybir.ActivationFunctionType
+ALU = mybir.AluOpType
+
+P = 128
+PACK = 4
+K_PASS = P * PACK
+BATCH, UNITS, ACTIONS = 1024, 1024, 128
+TILES = BATCH // P
+BATCH_TILES = TILES // 2
+PASSES = UNITS // K_PASS
+BANK = 512
+HALVES = UNITS // BANK
+BLOCKS = UNITS // P
+LN_EPS = 1e-5
+QUARTER = 0.25
+SMALLEST = 2.0 ** -60
+
+FLOPS = 2 * BATCH * UNITS * UNITS + 2 * BATCH * UNITS * ACTIONS
+
+
+def tile_actorflowode_pb_kernel(tc, h0, z, k1, W1, b1, ln1_g, ln1_b, W2, b2, out):
+    nc = tc.nc
+    with ExitStack() as ctx:
+        keep = ctx.enter_context(tc.tile_pool(name="keep", bufs=1))
+        stage = ctx.enter_context(tc.tile_pool(name="stage", bufs=2))
+        psum = ctx.enter_context(tc.psum_pool(name="psum", bufs=7))
+        psum_head = ctx.enter_context(tc.psum_pool(name="psum_head", bufs=1))
+        ctx.enter_context(tc.manual_schedule())
+
+        smallest = keep.tile([P, 1], F32)
+        nc.vector.memset(smallest[:], SMALLEST)
+        neg_half = keep.tile([P, 2], F32)
+        nc.vector.memset(neg_half[:], -0.5)
+        eps = keep.tile([P, 1], F32)
+        nc.vector.memset(eps[:], LN_EPS)
+        ones = keep.tile([P, P], BF16)
+        nc.vector.memset(ones[:], 1.0)
+        bias_rows = keep.tile([P, UNITS + 2 * ACTIONS], BF16)
+        nc.vector.memset(bias_rows[:], 0.0)
+        norm_rows = keep.tile([P, K_PASS], BF16)
+        nc.vector.memset(norm_rows[:], 0.0)
+        ident_f32 = keep.tile([P, P], F32)
+        make_identity(nc, ident_f32[:])
+        ident_bf16 = keep.tile([P, P], BF16)
+        make_identity(nc, ident_bf16[:])
+
+        nc.scalar.dma_start(out=bias_rows[0:1, 0:UNITS], in_=b1.rearrange("(o n) -> o n", o=1))
+        nc.scalar.dma_start(
+            out=bias_rows[0:1, UNITS : UNITS + ACTIONS], in_=b2.rearrange("(o n) -> o n", o=1)
+        )
+        nc.scalar.dma_start(out=norm_rows[0:PASSES, :], in_=ln1_g.rearrange("(c n) -> c n", n=K_PASS))
+        nc.scalar.dma_start(
+            out=norm_rows[PASSES : 2 * PASSES, :], in_=ln1_b.rearrange("(c n) -> c n", n=K_PASS)
+        )
+
+        warm = keep.tile([P, 1], F32)
+        nc.scalar.activation(out=warm[:], in_=smallest[:], func=FUNC.Sigmoid)
+
+        w1_raw = keep.tile([P, PASSES, PACK, UNITS], BF16)
+
+        def load_w1(half, g):
+            cols = slice(BANK * half, BANK * (half + 1))
+            nc.sync.dma_start(
+                out=w1_raw[:, g, :, cols],
+                in_=W1[K_PASS * g : K_PASS * (g + 1), cols].rearrange("(p t) n -> p t n", t=PACK),
+            )
+
+        h0_raw = [keep.tile([P, UNITS], BF16, name="h0_raw%d" % i) for i in range(TILES)]
+
+        def load_h0(i):
+            nc.sync.dma_start(out=h0_raw[i][:], in_=h0[P * i : P * (i + 1), :])
+
+        for half in range(HALVES):
+            for g in range(PASSES):
+                load_w1(half, g)
+        for i in range(TILES):
+            load_h0(i)
+        w2_raw = keep.tile([P, PASSES, PACK, ACTIONS], BF16)
+        nc.sync.dma_start(out=w2_raw[:], in_=W2.rearrange("(c p t) a -> p c t a", p=P, t=PACK))
+        z_rows = keep.tile([P, TILES, ACTIONS], BF16)
+        nc.sync.dma_start(out=z_rows[:], in_=z.rearrange("(i p) a -> p i a", p=P))
+        k1_rows = keep.tile([P, TILES, ACTIONS], BF16)
+        nc.sync.dma_start(out=k1_rows[:], in_=k1.rearrange("(i p) a -> p i a", p=P))
+
+        bias1 = keep.tile([P, UNITS], BF16)
+        for half in range(HALVES):
+            cols = slice(BANK * half, BANK * (half + 1))
+            spread = psum.tile([P, BANK], F32, tag="bank")
+            nc.tensor.matmul(out=spread[:], lhsT=ones[:], rhs=bias_rows[:, cols], start=True, stop=True)
+            nc.scalar.copy(
+                out=bias1[:, cols].rearrange("p (t m) -> p t m", t=PACK),
+                in_=spread[:].rearrange("p (m t) -> p t m", t=PACK),
+            )
+        bias2 = keep.tile([P, ACTIONS], F32)
+        spread = psum.tile([P, 2 * ACTIONS], F32, tag="bank")
+        nc.tensor.matmul(out=spread[:], lhsT=ones[:], rhs=bias_rows[:, UNITS:], start=True, stop=True)
+        nc.scalar.copy(out=bias2[:], in_=spread[:, 0:ACTIONS])
+        norm_split = keep.tile([P, PACK, P], BF16)
+        nc.scalar.copy(out=norm_split[:], in_=norm_rows[:].rearrange("r (m t) -> r t m", t=PACK))
+        norm_cols = psum.tile([P, PACK, P], BF16, tag="bank")
+        for t in range(PACK):
+            nc.tensor.transpose(norm_cols[:, t, :], norm_split[:, t, :], ident_bf16[:])
+        gain = keep.tile([P, BLOCKS], F32)
+        nc.scalar.copy(
+            out=gain[:].rearrange("p (c t) -> p c t", t=PACK),
+            in_=norm_cols[:, :, 0:PASSES].rearrange("p t c -> p c t"),
+        )
+        shift = keep.tile([P, BLOCKS], F32)
+        nc.scalar.copy(
+            out=shift[:].rearrange("p (c t) -> p c t", t=PACK),
+            in_=norm_cols[:, :, PASSES : 2 * PASSES].rearrange("p t c -> p c t"),
+        )
+
+        start_state = keep.tile([P, TILES, ACTIONS], F32)
+        slope = keep.tile([P, TILES, ACTIONS], F32)
+        nc.gpsimd.tensor_tensor(
+            out=slope[:], in0=k1_rows[:], in1=bias2[:].unsqueeze(1).to_broadcast([P, TILES, ACTIONS]),
+            op=ALU.add,
+        )
+        nc.gpsimd.tensor_scalar(
+            out=slope[:], in0=slope[:], scalar1=QUARTER, scalar2=0.0, op0=ALU.mult, op1=ALU.add
+        )
+        nc.gpsimd.tensor_tensor(out=start_state[:], in0=slope[:], in1=z_rows[:], op=ALU.add)
+
+        w1_codes = keep.tile([P, PASSES, UNITS], U32, align_bytes=64)
+        w1_scales = keep.tile([P, PASSES, UNITS], U8, align_bytes=64)
+        w1_grouped = {}
+
+        def regroup_w1(half, g):
+            cols = slice(BANK * half, BANK * (half + 1))
+            grouped = keep.tile([P, BANK, PACK], BF16, align_bytes=64, name="w1_grouped%d%d" % (half, g))
+            nc.vector.tensor_copy(
+                out=grouped[:].rearrange("p (c i) t -> p c t i", i=4),
+                in_=w1_raw[:, g, :, cols].rearrange("p t (c i) -> p c t i", i=4),
+            )
+            w1_grouped[(half, g)] = grouped
+
+        def quantise_w1(half, g):
+            cols = slice(BANK * half, BANK * (half + 1))
+            nc.vector.quantize_mx(
+                out=w1_codes[:, g, cols].bitcast(FP8X4),
+                scales=w1_scales[:, g, cols],
+                in_=w1_grouped[(half, g)][:].rearrange("p n t -> p (n t)"),
+            )
+
+        regroup_w1(0, 0)
+        regroup_w1(0, 1)
+        quantise_w1(0, 0)
+        regroup_w1(1, 0)
+        quantise_w1(0, 1)
+        regroup_w1(1, 1)
+        quantise_w1(1, 0)
+        quantise_w1(1, 1)
+
+        h0_codes = keep.tile([P, TILES, PASSES * P], U32, align_bytes=64)
+        h0_scales = keep.tile([P, TILES, PASSES * P], U8, align_bytes=64)
+        h0_grouped = [
+            keep.tile([P, UNITS], BF16, align_bytes=64, name="h0_grouped%d" % i) for i in range(TILES)
+        ]
+        pre_batch = [keep.tile([P, BATCH_TILES, UNITS], F32, name="pre_batch%d" % n) for n in range(2)]
+        work_batch = [keep.tile([P, BATCH_TILES, UNITS], F32, name="work_batch%d" % n) for n in range(2)]
+        pre = [pre_batch[i // BATCH_TILES][:, i % BATCH_TILES, :] for i in range(TILES)]
+        work = [work_batch[i // BATCH_TILES][:, i % BATCH_TILES, :] for i in range(TILES)]
+
+        def transpose_h0(i, copy):
+            words = h0_raw[i][:].bitcast(F32)
+            flipped = psum.tile([P, PACK, P], F32, tag="bank")
+            for g in range(PASSES):
+                for u in range(2):
+                    nc.tensor.transpose(
+                        flipped[:, 2 * g + u, :], words[:, 2 * P * g + u : 2 * P * (g + 1) : 2], ident_f32[:]
+                    )
+            copy(
+                out=h0_grouped[i][:].bitcast(F32).rearrange("p (g b u) -> p g b u", g=PASSES, u=2),
+                in_=flipped[:].rearrange("p (g u) b -> p g b u", u=2),
+            )
+
+        def quantise_h0(i):
+            nc.vector.quantize_mx(
+                out=h0_codes[:, i, :].bitcast(FP8X4), scales=h0_scales[:, i, :], in_=h0_grouped[i][:]
+            )
+
+        def first_product(i):
+            for half in range(HALVES):
+                cols = slice(BANK * half, BANK * (half + 1))
+                acc = psum.tile([P, BANK], F32, tag="bank")
+                for g in range(PASSES):
+                    rows = slice(P * g, P * (g + 1))
+                    nc.tensor.matmul_mx(
+                        out=acc[:],
+                        lhsT=h0_codes[:, i, rows].bitcast(FP8X4),
+                        lhsT_scale=h0_scales[:, i, rows],
+                        rhs=w1_codes[:, g, cols].bitcast(FP8X4),
+                        rhs_scale=w1_scales[:, g, cols],
+                        start=(g == 0),
+                        stop=(g == PASSES - 1),
+                    )
+                nc.vector.tensor_tensor(
+                    out=pre[i][:, cols].rearrange("p (t m) -> p t m", t=PACK),
+                    in0=acc[:].rearrange("p (m t) -> p t m", t=PACK),
+                    in1=bias1[:, cols].rearrange("p (t m) -> p t m", t=PACK),
+                    op=ALU.add,
+                )
+
+        def prepare(batch, copy):
+            for i in batch:
+                transpose_h0(i, copy)
+            for i in batch:
+                quantise_h0(i)
+            for i in batch:
+                first_product(i)
+
+        def sigmoid(values, result):
+            nc.scalar.activation(out=result, in_=values, func=FUNC.Sigmoid, scale=-1.0)
+
+        def log(n):
+            nc.scalar.activation(out=work_batch[n][:], in_=work_batch[n][:], func=FUNC.Ln, bias=smallest[:])
+
+        def tanh(i):
+            nc.scalar.activation(out=work[i], in_=work[i], func=FUNC.Tanh, scale=-1.0)
+
+        def mish(i, row_sum=None):
+            nc.vector.scalar_tensor_tensor(
+                out=pre[i], in0=pre[i], scalar=1.0, in1=work[i],
+                op0=ALU.mult, op1=ALU.mult, accum_out=row_sum,
+            )
+
+        mean = {}
+        inv_std = {}
+        moments = {}
+
+        def tiles_of(pair):
+            return (2 * pair, 2 * pair + 1)
+
+        def inverse_std(pair, padded):
+            both = keep.tile([P, 2], F32, name="inv_std%d" % pair)
+            nc.gpsimd.tensor_tensor(out=both[:], in0=padded[:], in1=neg_half[:], op=ALU.pow)
+            for k, i in enumerate(tiles_of(pair)):
+                inv_std[i] = both[:, k : k + 1]
+
+        parts = {}
+
+        def partial_moments(i):
+            parts[i] = keep.tile([P, HALVES, 6], F32, name="parts%d" % i)
+            for half in range(HALVES):
+                nc.vector.bn_stats(out=parts[i][:, half, :], in_=pre[i][:, BANK * half : BANK * (half + 1)])
+
+        def join_moments(i):
+            pair, k = i // 2, i % 2
+            if k == 0:
+                moments[pair] = keep.tile([P, 2, 2], F32, name="moments%d" % pair)
+            nc.vector.bn_aggr(out=moments[pair][:, k, :], in_=parts[i][:].rearrange("p h s -> p (h s)"))
+            mean[i] = moments[pair][:, k, 0:1]
+
+        def inverse_std_after_vector(pair):
+            padded = keep.tile([P, 2], F32, name="padded%d" % pair)
+            nc.vector.tensor_scalar_add(out=padded[:], in0=moments[pair][:, :, 1], scalar1=LN_EPS)
+            inverse_std(pair, padded)
+
+        def statistics_on_scalar(pair, row_sums):
+            squares = keep.tile([P, 2], F32, name="squares%d" % pair)
+            for k, i in enumerate(tiles_of(pair)):
+                nc.scalar.activation(
+                    out=work[i], in_=pre[i], func=FUNC.Square, bias=row_sums[:, k : k + 1],
+                    scale=-1.0 * UNITS, accum_out=squares[:, k : k + 1],
+                )
+            means = keep.tile([P, 2], F32, name="means%d" % pair)
+            nc.scalar.mul(out=means[:], in_=row_sums[:], mul=1.0 / UNITS)
+            for k, i in enumerate(tiles_of(pair)):
+                mean[i] = means[:, k : k + 1]
+            padded = keep.tile([P, 2], F32, name="padded%d" % pair)
+            nc.scalar.activation(
+                out=padded[:], in_=squares[:], func=FUNC.Identity, bias=eps[:], scale=1.0 / UNITS ** 3
+            )
+            inverse_std(pair, padded)
+
+        def normalise(i):
+            nc.vector.tensor_scalar(
+                out=work[i], in0=pre[i], scalar1=mean[i], scalar2=inv_std[i],
+                op0=ALU.subtract, op1=ALU.mult,
+            )
+
+        flipped = {}
+
+        def flip_hidden(i):
+            pair, place = i // 2, slice(P * (i % 2), P * (i % 2 + 1))
+            if i % 2 == 0:
+                flipped[pair] = [
+                    psum.tile([P, 2, 2 * P], F32, tag="bank", name="flipped%d" % k) for k in range(BLOCKS // 2)
+                ]
+            for j in range(BLOCKS):
+                nc.tensor.transpose(
+                    flipped[pair][j // 2][:, j % 2, place], work[i][:, P * j : P * (j + 1)], ident_f32[:]
+                )
+
+        planes = {}
+
+        def scale_pair(pair, c, on_scalar):
+            if c == 0:
+                planes[pair] = stage.tile([P, BLOCKS, 2 * P], BF16, tag="planes", name="planes")
+            for j in range(PACK * c, PACK * (c + 1)):
+                source = flipped[pair][j // 2][:, j % 2, :]
+                if on_scalar:
+                    nc.scalar.activation(
+                        out=planes[pair][:, j, :], in_=source, func=FUNC.Identity,
+                        bias=shift[:, j : j + 1], scale=gain[:, j : j + 1],
+                    )
+                else:
+                    nc.vector.tensor_scalar(
+                        out=planes[pair][:, j, :], in0=source,
+                        scalar1=gain[:, j : j + 1], scalar2=shift[:, j : j + 1],
+                        op0=ALU.mult, op1=ALU.add,
+                    )
+
+        w2_codes = keep.tile([P, PASSES * ACTIONS], U32, align_bytes=64)
+        w2_scales = keep.tile([P, PASSES * ACTIONS], U8, align_bytes=64)
+
+        def quantise_w2():
+            w2_grouped = keep.tile([P, PASSES, ACTIONS, PACK], BF16, align_bytes=64)
+            nc.vector.tensor_copy(
+                out=w2_grouped[:], in_=w2_raw[:].rearrange("p c t a -> p c a t")
+            )
+            nc.vector.quantize_mx(
+                out=w2_codes[:].bitcast(FP8X4), scales=w2_scales[:],
+                in_=w2_grouped[:].rearrange("p c a t -> p (c a t)"),
+            )
+
+        head_sums = {}
+
+        h1_grouped = {}
+
+        def regroup(pair):
+            grouped = stage.tile([P, PASSES, 2 * P, PACK], BF16, align_bytes=64, tag="h1_grouped")
+            for c in range(PASSES):
+                nc.vector.tensor_copy(
+                    out=grouped[:, c, :, :].rearrange("p (c i) t -> p c t i", i=4),
+                    in_=planes[pair][:, PACK * c : PACK * (c + 1), :].rearrange("p t (c i) -> p c t i", i=4),
+                )
+            h1_grouped[pair] = grouped
+
+        def second_product(pair):
+            grouped = h1_grouped[pair]
+            codes = stage.tile([P, PASSES, 2 * P], U32, align_bytes=64, tag="h1_codes")
+            scales = stage.tile([P, PASSES, 2 * P], U8, align_bytes=64, tag="h1_scales")
+            nc.vector.quantize_mx(
+                out=codes[:].rearrange("p c b -> p (c b)").bitcast(FP8X4),
+                scales=scales[:].rearrange("p c b -> p (c b)"),
+                in_=grouped[:].rearrange("p c b t -> p (c b t)"),
+            )
+            if pair % 2 == 0:
+                head_sums[pair // 2] = psum_head.tile([P, 4, ACTIONS], F32, tag="head", name="head_sums")
+            for r in range(2):
+                rows = slice(P * r, P * (r + 1))
+                for c in range(PASSES):
+                    cols = slice(ACTIONS * c, ACTIONS * (c + 1))
+                    nc.tensor.matmul_mx(
+                        out=head_sums[pair // 2][:, 2 * (pair % 2) + r, :],
+                        lhsT=codes[:, c, rows].bitcast(FP8X4),
+                        lhsT_scale=scales[:, c, rows],
+                        rhs=w2_codes[:, cols].bitcast(FP8X4),
+                        rhs_scale=w2_scales[:, cols],
+                        start=(c == 0),
+                        stop=(c == PASSES - 1),
+                    )
+
+        def corrector(pair):
+            result = stage.tile([P, 2, ACTIONS], F32, tag="result")
+            nc.vector.scalar_tensor_tensor(
+                out=result[:], in0=head_sums[pair // 2][:, 2 * (pair % 2) : 2 * (pair % 2) + 2, :], scalar=QUARTER,
+                in1=start_state[:, 2 * pair : 2 * pair + 2, :], op0=ALU.mult, op1=ALU.add,
+            )
+            nc.sync.dma_start(
+                out=out[2 * P * pair : 2 * P * (pair + 1), :].rearrange("(r p) a -> p r a", p=P),
+                in_=result[:],
+            )
+
+        first, last = range(0, BATCH_TILES), range(BATCH_TILES, TILES)
+        pair_a, pair_b = 0, 1
+        pair_c, pair_d = 2, 3
+        prepare(first, nc.scalar.copy)
+        for i in first:
+            sigmoid(pre[i], work[i])
+        prepare(last, nc.vector.tensor_copy)
+        quantise_w2()
+        log(0)
+        nc.scalar.activation(out=warm[:], in_=smallest[:], func=FUNC.Sigmoid)
+        for i in first:
+            tanh(i)
+            mish(i)
+            if i - 2 in first:
+                join_moments(i - 2)
+            if i - 1 in first:
+                partial_moments(i - 1)
+        sigmoid(pre_batch[1][:], work_batch[1][:])
+        log(1)
+        inverse_std_after_vector(pair_a)
+        partial_moments(3)
+        join_moments(2)
+        normalise(0)
+        flip_hidden(0)
+        join_moments(3)
+        normalise(1)
+        flip_hidden(1)
+        inverse_std_after_vector(pair_b)
+        normalise(2)
+        flip_hidden(2)
+        normalise(3)
+        flip_hidden(3)
+        for c in range(PASSES):
+            scale_pair(pair_a, c, on_scalar=False)
+        regroup(pair_a)
+        row_sums = {pair: keep.tile([P, 2], F32, name="row_sums%d" % pair) for pair in (pair_c, pair_d)}
+        for i in last:
+            tanh(i)
+            mish(i, row_sum=row_sums[i // 2][:, i % 2 : i % 2 + 1])
+            if i == last[0]:
+                second_product(pair_a)
+        statistics_on_scalar(pair_c, row_sums[pair_c])
+        scale_pair(pair_b, 0, on_scalar=False)
+        statistics_on_scalar(pair_d, row_sums[pair_d])
+        scale_pair(pair_b, 1, on_scalar=True)
+        for i in tiles_of(pair_c):
+            normalise(i)
+            flip_hidden(i)
+        corrector(pair_a)
+        for i in tiles_of(pair_d):
+            normalise(i)
+            flip_hidden(i)
+        regroup(pair_b)
+        second_product(pair_b)
+        for pair in (pair_c, pair_d):
+            for c in range(PASSES):
+                scale_pair(pair, c, on_scalar=True)
+            regroup(pair)
+            corrector(pair - 1)
+            second_product(pair)
+        corrector(pair_d)

@@ -16,7 +16,8 @@ PACK = 4
 K_PASS = P * PACK
 BATCH, UNITS, ACTIONS = 1024, 1024, 128
 TILES = BATCH // P
-BATCH_TILES = TILES // 2
+BATCHES = ((0, 1, 2, 3), (4, 5, 6, 7))
+GROUPS = ((0, 1), (2, 3), (4, 5), (6, 7))
 PASSES = UNITS // K_PASS
 BANK = 512
 HALVES = UNITS // BANK
@@ -32,157 +33,178 @@ def tile_actorflowode_pb_kernel(tc, h0, z, k1, W1, b1, ln1_g, ln1_b, W2, b2, out
     nc = tc.nc
     with ExitStack() as ctx:
         keep = ctx.enter_context(tc.tile_pool(name="keep", bufs=1))
-        stage = ctx.enter_context(tc.tile_pool(name="stage", bufs=2))
         psum = ctx.enter_context(tc.psum_pool(name="psum", bufs=7))
         psum_head = ctx.enter_context(tc.psum_pool(name="psum_head", bufs=1))
         ctx.enter_context(tc.manual_schedule())
 
         smallest = keep.tile([P, 1], F32)
         nc.vector.memset(smallest[:], SMALLEST)
+        ones = keep.tile([P, P], BF16)
+        nc.vector.memset(ones[:], 1.0)
+        bias_rows = keep.tile([P, UNITS], BF16)
+        nc.vector.memset(bias_rows[:], 0.0)
+        b2_rows = keep.tile([P, PACK, ACTIONS], BF16)
+        nc.vector.memset(b2_rows[:], 0.0)
+        norm_split = keep.tile([P, PACK, P], BF16)
+        nc.vector.memset(norm_split[:], 0.0)
         neg_half = keep.tile([P, 2], F32)
         nc.vector.memset(neg_half[:], -0.5)
         eps = keep.tile([P, 1], F32)
         nc.vector.memset(eps[:], LN_EPS)
-        ones = keep.tile([P, P], BF16)
-        nc.vector.memset(ones[:], 1.0)
-        bias_rows = keep.tile([P, UNITS + 2 * ACTIONS], BF16)
-        nc.vector.memset(bias_rows[:], 0.0)
-        norm_rows = keep.tile([P, K_PASS], BF16)
-        nc.vector.memset(norm_rows[:], 0.0)
         ident_f32 = keep.tile([P, P], F32)
         make_identity(nc, ident_f32[:])
-        ident_bf16 = keep.tile([P, P], BF16)
-        make_identity(nc, ident_bf16[:])
 
-        nc.scalar.dma_start(out=bias_rows[0:1, 0:UNITS], in_=b1.rearrange("(o n) -> o n", o=1))
-        nc.scalar.dma_start(
-            out=bias_rows[0:1, UNITS : UNITS + ACTIONS], in_=b2.rearrange("(o n) -> o n", o=1)
-        )
+        b1_row = keep.tile([1, UNITS], BF16)
+        nc.scalar.dma_start(out=b1_row[:], in_=b1.rearrange("(o n) -> o n", o=1))
+        norm_rows = keep.tile([2 * PASSES, K_PASS], BF16)
         nc.scalar.dma_start(out=norm_rows[0:PASSES, :], in_=ln1_g.rearrange("(c n) -> c n", n=K_PASS))
         nc.scalar.dma_start(
             out=norm_rows[PASSES : 2 * PASSES, :], in_=ln1_b.rearrange("(c n) -> c n", n=K_PASS)
         )
-
+        b2_row = keep.tile([1, ACTIONS], BF16)
+        nc.scalar.dma_start(out=b2_row[:], in_=b2.rearrange("(o n) -> o n", o=1))
         warm = keep.tile([P, 1], F32)
         nc.scalar.activation(out=warm[:], in_=smallest[:], func=FUNC.Sigmoid)
+        ident_bf16 = keep.tile([P, P], BF16)
+        nc.scalar.copy(out=ident_bf16[:], in_=ident_f32[:])
+        four_bf16 = keep.tile([P, P], BF16)
+        nc.scalar.mul(out=four_bf16[:], in_=ident_f32[:], mul=4.0)
+        nc.scalar.copy(out=bias_rows[0:1, :], in_=b1_row[:])
+        nc.scalar.copy(
+            out=norm_split[0 : 2 * PASSES, :, :], in_=norm_rows[:].rearrange("r (m t) -> r t m", t=PACK)
+        )
+        nc.scalar.copy(out=b2_rows[0:1, :, :], in_=b2_row[:].unsqueeze(1).to_broadcast([1, PACK, ACTIONS]))
 
-        w1_raw = keep.tile([P, PASSES, PACK, UNITS], BF16)
+        w1_raw = {}
 
         def load_w1(half, g):
             cols = slice(BANK * half, BANK * (half + 1))
+            raw = keep.tile([P, PACK, BANK], BF16, name="w1_raw%d%d" % (half, g))
             nc.sync.dma_start(
-                out=w1_raw[:, g, :, cols],
-                in_=W1[K_PASS * g : K_PASS * (g + 1), cols].rearrange("(p t) n -> p t n", t=PACK),
+                out=raw[:], in_=W1[K_PASS * g : K_PASS * (g + 1), cols].rearrange("(p t) n -> p t n", t=PACK)
             )
+            w1_raw[(half, g)] = raw
 
-        h0_raw = [keep.tile([P, UNITS], BF16, name="h0_raw%d" % i) for i in range(TILES)]
+        h0_raw = {}
 
         def load_h0(i):
+            h0_raw[i] = keep.tile([P, UNITS], BF16, name="h0_raw%d" % i)
             nc.sync.dma_start(out=h0_raw[i][:], in_=h0[P * i : P * (i + 1), :])
 
-        for half in range(HALVES):
-            for g in range(PASSES):
-                load_w1(half, g)
-        for i in range(TILES):
-            load_h0(i)
-        w2_raw = keep.tile([P, PASSES, PACK, ACTIONS], BF16)
-        nc.sync.dma_start(out=w2_raw[:], in_=W2.rearrange("(c p t) a -> p c t a", p=P, t=PACK))
         z_rows = keep.tile([P, TILES, ACTIONS], BF16)
-        nc.sync.dma_start(out=z_rows[:], in_=z.rearrange("(i p) a -> p i a", p=P))
         k1_rows = keep.tile([P, TILES, ACTIONS], BF16)
+        w2_raw = keep.tile([P, PASSES, PACK, ACTIONS], BF16)
+        load_w1(0, 0)
+        load_w1(0, 1)
+        load_h0(0)
+        load_h0(1)
+        load_w1(1, 0)
+        load_w1(1, 1)
+        load_h0(2)
+        load_h0(3)
+        for i in range(4, TILES):
+            load_h0(i)
+        nc.sync.dma_start(out=w2_raw[:], in_=W2.rearrange("(c p t) a -> p c t a", p=P, t=PACK))
+        nc.sync.dma_start(out=z_rows[:], in_=z.rearrange("(i p) a -> p i a", p=P))
         nc.sync.dma_start(out=k1_rows[:], in_=k1.rearrange("(i p) a -> p i a", p=P))
 
         bias1 = keep.tile([P, UNITS], BF16)
-        for half in range(HALVES):
+
+        def spread_b1(half):
             cols = slice(BANK * half, BANK * (half + 1))
-            spread = psum.tile([P, BANK], F32, tag="bank")
+            spread = psum.tile([P, BANK], F32, tag="bank", name="spread")
             nc.tensor.matmul(out=spread[:], lhsT=ones[:], rhs=bias_rows[:, cols], start=True, stop=True)
             nc.scalar.copy(
                 out=bias1[:, cols].rearrange("p (t m) -> p t m", t=PACK),
                 in_=spread[:].rearrange("p (m t) -> p t m", t=PACK),
             )
-        bias2 = keep.tile([P, ACTIONS], F32)
-        spread = psum.tile([P, 2 * ACTIONS], F32, tag="bank")
-        nc.tensor.matmul(out=spread[:], lhsT=ones[:], rhs=bias_rows[:, UNITS:], start=True, stop=True)
-        nc.scalar.copy(out=bias2[:], in_=spread[:, 0:ACTIONS])
-        norm_split = keep.tile([P, PACK, P], BF16)
-        nc.scalar.copy(out=norm_split[:], in_=norm_rows[:].rearrange("r (m t) -> r t m", t=PACK))
-        norm_cols = psum.tile([P, PACK, P], BF16, tag="bank")
-        for t in range(PACK):
-            nc.tensor.transpose(norm_cols[:, t, :], norm_split[:, t, :], ident_bf16[:])
+
+        small = {}
         gain = keep.tile([P, BLOCKS], F32)
-        nc.scalar.copy(
-            out=gain[:].rearrange("p (c t) -> p c t", t=PACK),
-            in_=norm_cols[:, :, 0:PASSES].rearrange("p t c -> p c t"),
-        )
         shift = keep.tile([P, BLOCKS], F32)
-        nc.scalar.copy(
-            out=shift[:].rearrange("p (c t) -> p c t", t=PACK),
-            in_=norm_cols[:, :, PASSES : 2 * PASSES].rearrange("p t c -> p c t"),
-        )
+
+        def norm_columns():
+            norm_cols = psum.tile([P, PACK, P], BF16, tag="bank", name="norm_cols")
+            for t in range(PACK):
+                nc.tensor.transpose(norm_cols[:, t, :], norm_split[:, t, :], ident_bf16[:])
+            small["norm_cols"] = norm_cols
+
+        def copy_norm_columns():
+            norm_cols = small["norm_cols"]
+            nc.scalar.copy(
+                out=gain[:].rearrange("p (c t) -> p c t", t=PACK),
+                in_=norm_cols[:, :, 0:PASSES].rearrange("p t c -> p c t"),
+            )
+            nc.scalar.copy(
+                out=shift[:].rearrange("p (c t) -> p c t", t=PACK),
+                in_=norm_cols[:, :, PASSES : 2 * PASSES].rearrange("p t c -> p c t"),
+            )
 
         start_state = keep.tile([P, TILES, ACTIONS], F32)
-        slope = keep.tile([P, TILES, ACTIONS], F32)
-        nc.gpsimd.tensor_tensor(
-            out=slope[:], in0=k1_rows[:], in1=bias2[:].unsqueeze(1).to_broadcast([P, TILES, ACTIONS]),
-            op=ALU.add,
-        )
-        nc.gpsimd.tensor_scalar(
-            out=slope[:], in0=slope[:], scalar1=QUARTER, scalar2=0.0, op0=ALU.mult, op1=ALU.add
-        )
-        nc.gpsimd.tensor_tensor(out=start_state[:], in0=slope[:], in1=z_rows[:], op=ALU.add)
 
-        w1_codes = keep.tile([P, PASSES, UNITS], U32, align_bytes=64)
-        w1_scales = keep.tile([P, PASSES, UNITS], U8, align_bytes=64)
+        def make_start_state():
+            for n in range(2):
+                tiles = slice(PACK * n, PACK * (n + 1))
+                total = psum.tile([P, PACK, ACTIONS], F32, tag="bank", name="total")
+                terms = ((four_bf16, z_rows[:, tiles, :]), (ident_bf16, k1_rows[:, tiles, :]), (ones, b2_rows[:]))
+                for k, (left, right) in enumerate(terms):
+                    nc.tensor.matmul(
+                        out=total[:].rearrange("p i a -> p (i a)"), lhsT=left[:],
+                        rhs=right.rearrange("p i a -> p (i a)"), start=(k == 0), stop=(k == 2),
+                    )
+                small[n] = total
+
+        def copy_start_state():
+            for n in range(2):
+                tiles = slice(PACK * n, PACK * (n + 1))
+                nc.scalar.activation(out=start_state[:, tiles, :], in_=small[n][:], func=FUNC.Copy, scale=QUARTER)
+
+        w1_codes = {}
+        w1_scales = {}
         w1_grouped = {}
+        for half in range(HALVES):
+            for g in range(PASSES):
+                w1_codes[(half, g)] = keep.tile([P, BANK], U32, align_bytes=64, name="w1_codes%d%d" % (half, g))
+                w1_scales[(half, g)] = keep.tile([P, BANK], U8, align_bytes=64, name="w1_scales%d%d" % (half, g))
 
-        def regroup_w1(half, g):
-            cols = slice(BANK * half, BANK * (half + 1))
+        def regroup_w1(half, g, copy):
             grouped = keep.tile([P, BANK, PACK], BF16, align_bytes=64, name="w1_grouped%d%d" % (half, g))
-            nc.vector.tensor_copy(
+            copy(
                 out=grouped[:].rearrange("p (c i) t -> p c t i", i=4),
-                in_=w1_raw[:, g, :, cols].rearrange("p t (c i) -> p c t i", i=4),
+                in_=w1_raw[(half, g)][:].rearrange("p t (c i) -> p c t i", i=4),
             )
             w1_grouped[(half, g)] = grouped
 
         def quantise_w1(half, g):
-            cols = slice(BANK * half, BANK * (half + 1))
             nc.vector.quantize_mx(
-                out=w1_codes[:, g, cols].bitcast(FP8X4),
-                scales=w1_scales[:, g, cols],
+                out=w1_codes[(half, g)][:].bitcast(FP8X4), scales=w1_scales[(half, g)][:],
                 in_=w1_grouped[(half, g)][:].rearrange("p n t -> p (n t)"),
             )
 
-        regroup_w1(0, 0)
-        regroup_w1(0, 1)
-        quantise_w1(0, 0)
-        regroup_w1(1, 0)
-        quantise_w1(0, 1)
-        regroup_w1(1, 1)
-        quantise_w1(1, 0)
-        quantise_w1(1, 1)
-
         h0_codes = keep.tile([P, TILES, PASSES * P], U32, align_bytes=64)
         h0_scales = keep.tile([P, TILES, PASSES * P], U8, align_bytes=64)
-        h0_grouped = [
-            keep.tile([P, UNITS], BF16, align_bytes=64, name="h0_grouped%d" % i) for i in range(TILES)
-        ]
-        pre_batch = [keep.tile([P, BATCH_TILES, UNITS], F32, name="pre_batch%d" % n) for n in range(2)]
-        work_batch = [keep.tile([P, BATCH_TILES, UNITS], F32, name="work_batch%d" % n) for n in range(2)]
-        pre = [pre_batch[i // BATCH_TILES][:, i % BATCH_TILES, :] for i in range(TILES)]
-        work = [work_batch[i // BATCH_TILES][:, i % BATCH_TILES, :] for i in range(TILES)]
+        h0_grouped = {}
+        pre_batch, work_batch, pre, work = {}, {}, {}, {}
+        for n, batch in enumerate(BATCHES):
+            pre_batch[n] = keep.tile([P, len(batch), UNITS], F32, name="pre_batch%d" % n)
+            work_batch[n] = keep.tile([P, len(batch), UNITS], F32, name="work_batch%d" % n)
+            for k, i in enumerate(batch):
+                pre[i] = pre_batch[n][:, k, :]
+                work[i] = work_batch[n][:, k, :]
+        group_of = {i: (q, k) for q, group in enumerate(GROUPS) for k, i in enumerate(group)}
 
         def transpose_h0(i, copy):
             words = h0_raw[i][:].bitcast(F32)
-            flipped = psum.tile([P, PACK, P], F32, tag="bank")
+            turned = psum.tile([P, PACK, P], F32, tag="bank", name="turned")
             for g in range(PASSES):
                 for u in range(2):
                     nc.tensor.transpose(
-                        flipped[:, 2 * g + u, :], words[:, 2 * P * g + u : 2 * P * (g + 1) : 2], ident_f32[:]
+                        turned[:, 2 * g + u, :], words[:, 2 * P * g + u : 2 * P * (g + 1) : 2], ident_f32[:]
                     )
+            h0_grouped[i] = keep.tile([P, UNITS], BF16, align_bytes=64, name="h0_grouped%d" % i)
             copy(
                 out=h0_grouped[i][:].bitcast(F32).rearrange("p (g b u) -> p g b u", g=PASSES, u=2),
-                in_=flipped[:].rearrange("p (g u) b -> p g b u", u=2),
+                in_=turned[:].rearrange("p (g u) b -> p g b u", u=2),
             )
 
         def quantise_h0(i):
@@ -190,38 +212,33 @@ def tile_actorflowode_pb_kernel(tc, h0, z, k1, W1, b1, ln1_g, ln1_b, W2, b2, out
                 out=h0_codes[:, i, :].bitcast(FP8X4), scales=h0_scales[:, i, :], in_=h0_grouped[i][:]
             )
 
-        def first_product(i):
-            for half in range(HALVES):
-                cols = slice(BANK * half, BANK * (half + 1))
-                acc = psum.tile([P, BANK], F32, tag="bank")
-                for g in range(PASSES):
-                    rows = slice(P * g, P * (g + 1))
-                    nc.tensor.matmul_mx(
-                        out=acc[:],
-                        lhsT=h0_codes[:, i, rows].bitcast(FP8X4),
-                        lhsT_scale=h0_scales[:, i, rows],
-                        rhs=w1_codes[:, g, cols].bitcast(FP8X4),
-                        rhs_scale=w1_scales[:, g, cols],
-                        start=(g == 0),
-                        stop=(g == PASSES - 1),
-                    )
-                nc.vector.tensor_tensor(
-                    out=pre[i][:, cols].rearrange("p (t m) -> p t m", t=PACK),
-                    in0=acc[:].rearrange("p (m t) -> p t m", t=PACK),
-                    in1=bias1[:, cols].rearrange("p (t m) -> p t m", t=PACK),
-                    op=ALU.add,
+        acc = {}
+
+        def multiply(i, half):
+            acc[(i, half)] = psum.tile([P, BANK], F32, tag="bank", name="acc")
+            for g in range(PASSES):
+                rows = slice(P * g, P * (g + 1))
+                nc.tensor.matmul_mx(
+                    out=acc[(i, half)][:],
+                    lhsT=h0_codes[:, i, rows].bitcast(FP8X4), lhsT_scale=h0_scales[:, i, rows],
+                    rhs=w1_codes[(half, g)][:].bitcast(FP8X4), rhs_scale=w1_scales[(half, g)][:],
+                    start=(g == 0), stop=(g == PASSES - 1),
                 )
 
-        def prepare(batch, copy):
-            for i in batch:
-                transpose_h0(i, copy)
-            for i in batch:
-                quantise_h0(i)
-            for i in batch:
-                first_product(i)
+        def add_bias(i, half):
+            cols = slice(BANK * half, BANK * (half + 1))
+            nc.vector.tensor_tensor(
+                out=pre[i][:, cols].rearrange("p (t m) -> p t m", t=PACK),
+                in0=acc[(i, half)][:].rearrange("p (m t) -> p t m", t=PACK),
+                in1=bias1[:, cols].rearrange("p (t m) -> p t m", t=PACK),
+                op=ALU.add,
+            )
 
-        def sigmoid(values, result):
-            nc.scalar.activation(out=result, in_=values, func=FUNC.Sigmoid, scale=-1.0)
+        def sigmoid(i):
+            nc.scalar.activation(out=work[i], in_=pre[i], func=FUNC.Sigmoid, scale=-1.0)
+
+        def sigmoid_batch(n):
+            nc.scalar.activation(out=work_batch[n][:], in_=pre_batch[n][:], func=FUNC.Sigmoid, scale=-1.0)
 
         def log(n):
             nc.scalar.activation(out=work_batch[n][:], in_=work_batch[n][:], func=FUNC.Ln, bias=smallest[:])
@@ -229,26 +246,29 @@ def tile_actorflowode_pb_kernel(tc, h0, z, k1, W1, b1, ln1_g, ln1_b, W2, b2, out
         def tanh(i):
             nc.scalar.activation(out=work[i], in_=work[i], func=FUNC.Tanh, scale=-1.0)
 
-        def mish(i, row_sum=None):
+        row_sums = {}
+
+        def mish(i, with_sum):
+            q, k = group_of[i]
+            if with_sum and k == 0:
+                row_sums[q] = keep.tile([P, len(GROUPS[q])], F32, name="row_sums%d" % q)
             nc.vector.scalar_tensor_tensor(
-                out=pre[i], in0=pre[i], scalar=1.0, in1=work[i],
-                op0=ALU.mult, op1=ALU.mult, accum_out=row_sum,
+                out=pre[i], in0=pre[i], scalar=1.0, in1=work[i], op0=ALU.mult, op1=ALU.mult,
+                accum_out=row_sums[q][:, k : k + 1] if with_sum else None,
             )
 
         mean = {}
         inv_std = {}
         moments = {}
-
-        def tiles_of(pair):
-            return (2 * pair, 2 * pair + 1)
-
-        def inverse_std(pair, padded):
-            both = keep.tile([P, 2], F32, name="inv_std%d" % pair)
-            nc.gpsimd.tensor_tensor(out=both[:], in0=padded[:], in1=neg_half[:], op=ALU.pow)
-            for k, i in enumerate(tiles_of(pair)):
-                inv_std[i] = both[:, k : k + 1]
-
         parts = {}
+        squares = {}
+
+        def inverse_std(q, padded):
+            width = len(GROUPS[q])
+            result = keep.tile([P, width], F32, name="inv_std%d" % q)
+            nc.gpsimd.tensor_tensor(out=result[:], in0=padded[:], in1=neg_half[:, 0:width], op=ALU.pow)
+            for k, i in enumerate(GROUPS[q]):
+                inv_std[i] = result[:, k : k + 1]
 
         def partial_moments(i):
             parts[i] = keep.tile([P, HALVES, 6], F32, name="parts%d" % i)
@@ -256,154 +276,221 @@ def tile_actorflowode_pb_kernel(tc, h0, z, k1, W1, b1, ln1_g, ln1_b, W2, b2, out
                 nc.vector.bn_stats(out=parts[i][:, half, :], in_=pre[i][:, BANK * half : BANK * (half + 1)])
 
         def join_moments(i):
-            pair, k = i // 2, i % 2
+            q, k = group_of[i]
             if k == 0:
-                moments[pair] = keep.tile([P, 2, 2], F32, name="moments%d" % pair)
-            nc.vector.bn_aggr(out=moments[pair][:, k, :], in_=parts[i][:].rearrange("p h s -> p (h s)"))
-            mean[i] = moments[pair][:, k, 0:1]
+                moments[q] = keep.tile([P, len(GROUPS[q]), 2], F32, name="moments%d" % q)
+            nc.vector.bn_aggr(out=moments[q][:, k, :], in_=parts[i][:].rearrange("p h s -> p (h s)"))
+            mean[i] = moments[q][:, k, 0:1]
 
-        def inverse_std_after_vector(pair):
-            padded = keep.tile([P, 2], F32, name="padded%d" % pair)
-            nc.vector.tensor_scalar_add(out=padded[:], in0=moments[pair][:, :, 1], scalar1=LN_EPS)
-            inverse_std(pair, padded)
+        def inverse_std_after_vector(q):
+            padded = keep.tile([P, len(GROUPS[q])], F32, name="padded%d" % q)
+            nc.vector.tensor_scalar_add(out=padded[:], in0=moments[q][:, :, 1], scalar1=LN_EPS)
+            inverse_std(q, padded)
 
-        def statistics_on_scalar(pair, row_sums):
-            squares = keep.tile([P, 2], F32, name="squares%d" % pair)
-            for k, i in enumerate(tiles_of(pair)):
-                nc.scalar.activation(
-                    out=work[i], in_=pre[i], func=FUNC.Square, bias=row_sums[:, k : k + 1],
-                    scale=-1.0 * UNITS, accum_out=squares[:, k : k + 1],
-                )
-            means = keep.tile([P, 2], F32, name="means%d" % pair)
-            nc.scalar.mul(out=means[:], in_=row_sums[:], mul=1.0 / UNITS)
-            for k, i in enumerate(tiles_of(pair)):
-                mean[i] = means[:, k : k + 1]
-            padded = keep.tile([P, 2], F32, name="padded%d" % pair)
+        def square(i):
+            q, k = group_of[i]
+            if k == 0:
+                squares[q] = keep.tile([P, len(GROUPS[q])], F32, name="squares%d" % q)
             nc.scalar.activation(
-                out=padded[:], in_=squares[:], func=FUNC.Identity, bias=eps[:], scale=1.0 / UNITS ** 3
+                out=work[i], in_=pre[i], func=FUNC.Square, bias=row_sums[q][:, k : k + 1],
+                scale=-1.0 * UNITS, accum_out=squares[q][:, k : k + 1],
             )
-            inverse_std(pair, padded)
+
+        def inverse_std_after_scalar(q):
+            means = keep.tile([P, len(GROUPS[q])], F32, name="means%d" % q)
+            nc.scalar.mul(out=means[:], in_=row_sums[q][:], mul=1.0 / UNITS)
+            for k, i in enumerate(GROUPS[q]):
+                mean[i] = means[:, k : k + 1]
+            padded = keep.tile([P, len(GROUPS[q])], F32, name="padded%d" % q)
+            nc.scalar.activation(
+                out=padded[:], in_=squares[q][:], func=FUNC.Identity, bias=eps[:], scale=1.0 / UNITS ** 3
+            )
+            inverse_std(q, padded)
 
         def normalise(i):
             nc.vector.tensor_scalar(
-                out=work[i], in0=pre[i], scalar1=mean[i], scalar2=inv_std[i],
-                op0=ALU.subtract, op1=ALU.mult,
+                out=work[i], in0=pre[i], scalar1=mean[i], scalar2=inv_std[i], op0=ALU.subtract, op1=ALU.mult
             )
 
         flipped = {}
 
         def flip_hidden(i):
-            pair, place = i // 2, slice(P * (i % 2), P * (i % 2 + 1))
-            if i % 2 == 0:
-                flipped[pair] = [
-                    psum.tile([P, 2, 2 * P], F32, tag="bank", name="flipped%d" % k) for k in range(BLOCKS // 2)
-                ]
+            q, k = group_of[i]
+            width = P * len(GROUPS[q])
+            each = BANK // width
+            if k == 0:
+                flipped[q] = []
+                for n in range(BLOCKS // each):
+                    bank = psum.tile([P, each, width], F32, tag="bank", name="flipped%d" % n)
+                    flipped[q] += [bank[:, b, :] for b in range(each)]
             for j in range(BLOCKS):
                 nc.tensor.transpose(
-                    flipped[pair][j // 2][:, j % 2, place], work[i][:, P * j : P * (j + 1)], ident_f32[:]
+                    flipped[q][j][:, P * k : P * (k + 1)], work[i][:, P * j : P * (j + 1)], ident_f32[:]
                 )
 
         planes = {}
 
-        def scale_pair(pair, c, on_scalar):
-            if c == 0:
-                planes[pair] = stage.tile([P, BLOCKS, 2 * P], BF16, tag="planes", name="planes")
+        def scale_block(q, j, on_scalar):
+            if q not in planes:
+                planes[q] = keep.tile([P, BLOCKS, P * len(GROUPS[q])], BF16, name="planes%d" % q)
+            if on_scalar:
+                nc.scalar.activation(
+                    out=planes[q][:, j, :], in_=flipped[q][j], func=FUNC.Identity,
+                    bias=shift[:, j : j + 1], scale=gain[:, j : j + 1],
+                )
+            else:
+                nc.vector.tensor_scalar(
+                    out=planes[q][:, j, :], in0=flipped[q][j],
+                    scalar1=gain[:, j : j + 1], scalar2=shift[:, j : j + 1], op0=ALU.mult, op1=ALU.add,
+                )
+
+        def scale_pass(q, c, on_scalar):
             for j in range(PACK * c, PACK * (c + 1)):
-                source = flipped[pair][j // 2][:, j % 2, :]
-                if on_scalar:
-                    nc.scalar.activation(
-                        out=planes[pair][:, j, :], in_=source, func=FUNC.Identity,
-                        bias=shift[:, j : j + 1], scale=gain[:, j : j + 1],
-                    )
-                else:
-                    nc.vector.tensor_scalar(
-                        out=planes[pair][:, j, :], in0=source,
-                        scalar1=gain[:, j : j + 1], scalar2=shift[:, j : j + 1],
-                        op0=ALU.mult, op1=ALU.add,
-                    )
+                scale_block(q, j, on_scalar)
 
         w2_codes = keep.tile([P, PASSES * ACTIONS], U32, align_bytes=64)
         w2_scales = keep.tile([P, PASSES * ACTIONS], U8, align_bytes=64)
+        w2_grouped = keep.tile([P, PASSES, ACTIONS, PACK], BF16, align_bytes=64)
+
+        def regroup_w2(copy):
+            copy(out=w2_grouped[:], in_=w2_raw[:].rearrange("p c t a -> p c a t"))
 
         def quantise_w2():
-            w2_grouped = keep.tile([P, PASSES, ACTIONS, PACK], BF16, align_bytes=64)
-            nc.vector.tensor_copy(
-                out=w2_grouped[:], in_=w2_raw[:].rearrange("p c t a -> p c a t")
-            )
             nc.vector.quantize_mx(
                 out=w2_codes[:].bitcast(FP8X4), scales=w2_scales[:],
                 in_=w2_grouped[:].rearrange("p c a t -> p (c a t)"),
             )
 
-        head_sums = {}
+        grouped = {}
+        codes = {}
+        scales = {}
+        head_sums = psum_head.tile([P, PACK, ACTIONS], F32, name="head_sums")
 
-        h1_grouped = {}
-
-        def regroup(pair):
-            grouped = stage.tile([P, PASSES, 2 * P, PACK], BF16, align_bytes=64, tag="h1_grouped")
-            for c in range(PASSES):
-                nc.vector.tensor_copy(
-                    out=grouped[:, c, :, :].rearrange("p (c i) t -> p c t i", i=4),
-                    in_=planes[pair][:, PACK * c : PACK * (c + 1), :].rearrange("p t (c i) -> p c t i", i=4),
-                )
-            h1_grouped[pair] = grouped
-
-        def second_product(pair):
-            grouped = h1_grouped[pair]
-            codes = stage.tile([P, PASSES, 2 * P], U32, align_bytes=64, tag="h1_codes")
-            scales = stage.tile([P, PASSES, 2 * P], U8, align_bytes=64, tag="h1_scales")
-            nc.vector.quantize_mx(
-                out=codes[:].rearrange("p c b -> p (c b)").bitcast(FP8X4),
-                scales=scales[:].rearrange("p c b -> p (c b)"),
-                in_=grouped[:].rearrange("p c b t -> p (c b t)"),
+        def regroup(q, c):
+            rows = P * len(GROUPS[q])
+            if q not in grouped:
+                grouped[q] = keep.tile([P, PASSES, rows, PACK], BF16, align_bytes=64, name="h1_grouped%d" % q)
+                codes[q] = keep.tile([P, PASSES, rows], U32, align_bytes=64, name="h1_codes%d" % q)
+                scales[q] = keep.tile([P, PASSES, rows], U8, align_bytes=64, name="h1_scales%d" % q)
+            nc.vector.tensor_copy(
+                out=grouped[q][:, c, :, :].rearrange("p (c i) t -> p c t i", i=4),
+                in_=planes[q][:, PACK * c : PACK * (c + 1), :].rearrange("p t (c i) -> p c t i", i=4),
             )
-            if pair % 2 == 0:
-                head_sums[pair // 2] = psum_head.tile([P, 4, ACTIONS], F32, tag="head", name="head_sums")
-            for r in range(2):
-                rows = slice(P * r, P * (r + 1))
+
+        def quantise(q, c):
+            nc.vector.quantize_mx(
+                out=codes[q][:, c, :].bitcast(FP8X4), scales=scales[q][:, c, :],
+                in_=grouped[q][:, c, :, :].rearrange("p b t -> p (b t)"),
+            )
+
+        def second_product(q):
+            for k in range(len(GROUPS[q])):
+                rows = slice(P * k, P * (k + 1))
                 for c in range(PASSES):
                     cols = slice(ACTIONS * c, ACTIONS * (c + 1))
                     nc.tensor.matmul_mx(
-                        out=head_sums[pair // 2][:, 2 * (pair % 2) + r, :],
-                        lhsT=codes[:, c, rows].bitcast(FP8X4),
-                        lhsT_scale=scales[:, c, rows],
-                        rhs=w2_codes[:, cols].bitcast(FP8X4),
-                        rhs_scale=w2_scales[:, cols],
-                        start=(c == 0),
-                        stop=(c == PASSES - 1),
+                        out=head_sums[:, 2 * (q % 2) + k, :],
+                        lhsT=codes[q][:, c, rows].bitcast(FP8X4), lhsT_scale=scales[q][:, c, rows],
+                        rhs=w2_codes[:, cols].bitcast(FP8X4), rhs_scale=w2_scales[:, cols],
+                        start=(c == 0), stop=(c == PASSES - 1),
                     )
 
-        def corrector(pair):
-            result = stage.tile([P, 2, ACTIONS], F32, tag="result")
+        def corrector(q):
+            first, width = GROUPS[q][0], len(GROUPS[q])
+            slot = 2 * (q % 2)
+            result = keep.tile([P, width, ACTIONS], F32, name="result%d" % q)
             nc.vector.scalar_tensor_tensor(
-                out=result[:], in0=head_sums[pair // 2][:, 2 * (pair % 2) : 2 * (pair % 2) + 2, :], scalar=QUARTER,
-                in1=start_state[:, 2 * pair : 2 * pair + 2, :], op0=ALU.mult, op1=ALU.add,
+                out=result[:], in0=head_sums[:, slot : slot + width, :], scalar=QUARTER,
+                in1=start_state[:, first : first + width, :], op0=ALU.mult, op1=ALU.add,
             )
             nc.sync.dma_start(
-                out=out[2 * P * pair : 2 * P * (pair + 1), :].rearrange("(r p) a -> p r a", p=P),
+                out=out[P * first : P * (first + width), :].rearrange("(r p) a -> p r a", p=P),
                 in_=result[:],
             )
 
-        first, last = range(0, BATCH_TILES), range(BATCH_TILES, TILES)
-        pair_a, pair_b = 0, 1
-        pair_c, pair_d = 2, 3
-        prepare(first, nc.scalar.copy)
-        for i in first:
-            sigmoid(pre[i], work[i])
-        prepare(last, nc.vector.tensor_copy)
-        quantise_w2()
+
+        vcopy, scopy = nc.vector.tensor_copy, nc.scalar.copy
+        regroup_w1(0, 0, vcopy)
+        transpose_h0(0, scopy)
+        transpose_h0(1, scopy)
+        spread_b1(0)
+        spread_b1(1)
+        regroup_w1(0, 1, vcopy)
+        quantise_w1(0, 0)
+        quantise_h0(0)
+        quantise_w1(0, 1)
+        quantise_h0(1)
+        regroup_w1(1, 0, scopy)
+        regroup_w1(1, 1, vcopy)
+        multiply(0, 0)
+        multiply(1, 0)
+        transpose_h0(2, scopy)
+        transpose_h0(3, scopy)
+        add_bias(0, 0)
+        add_bias(1, 0)
+        quantise_w1(1, 1)
+        quantise_w1(1, 0)
+        multiply(0, 1)
+        multiply(1, 1)
+        quantise_h0(2)
+        add_bias(0, 1)
+        multiply(2, 0)
+        multiply(2, 1)
+        sigmoid(0)
+        quantise_h0(3)
+        add_bias(1, 1)
+        multiply(3, 0)
+        multiply(3, 1)
+        sigmoid(1)
+        add_bias(2, 0)
+        add_bias(2, 1)
+        sigmoid(2)
+        add_bias(3, 0)
+        add_bias(3, 1)
+        sigmoid(3)
         log(0)
         nc.scalar.activation(out=warm[:], in_=smallest[:], func=FUNC.Sigmoid)
-        for i in first:
+        for i in (4, 5, 6, 7):
+            transpose_h0(i, vcopy)
+        quantise_h0(4)
+        quantise_h0(5)
+        multiply(4, 0)
+        multiply(4, 1)
+        quantise_h0(6)
+        multiply(5, 0)
+        multiply(5, 1)
+        add_bias(4, 0)
+        quantise_h0(7)
+        add_bias(4, 1)
+        multiply(6, 0)
+        multiply(6, 1)
+        multiply(7, 0)
+        multiply(7, 1)
+        regroup_w2(vcopy)
+        add_bias(5, 0)
+        add_bias(5, 1)
+        quantise_w2()
+        add_bias(6, 0)
+        add_bias(6, 1)
+        add_bias(7, 0)
+        add_bias(7, 1)
+        norm_columns()
+        for i in range(4):
             tanh(i)
-            mish(i)
-            if i - 2 in first:
-                join_moments(i - 2)
-            if i - 1 in first:
-                partial_moments(i - 1)
-        sigmoid(pre_batch[1][:], work_batch[1][:])
+        copy_norm_columns()
+        sigmoid_batch(1)
         log(1)
-        inverse_std_after_vector(pair_a)
+
+        mish(0, False)
+        mish(1, False)
+        partial_moments(0)
+        mish(2, False)
+        partial_moments(1)
+        join_moments(0)
+        mish(3, False)
+        join_moments(1)
+        partial_moments(2)
+        inverse_std_after_vector(0)
         partial_moments(3)
         join_moments(2)
         normalise(0)
@@ -411,37 +498,64 @@ def tile_actorflowode_pb_kernel(tc, h0, z, k1, W1, b1, ln1_g, ln1_b, W2, b2, out
         join_moments(3)
         normalise(1)
         flip_hidden(1)
-        inverse_std_after_vector(pair_b)
+        inverse_std_after_vector(1)
+        scale_pass(0, 0, False)
+        scale_pass(0, 1, False)
         normalise(2)
         flip_hidden(2)
         normalise(3)
         flip_hidden(3)
-        for c in range(PASSES):
-            scale_pair(pair_a, c, on_scalar=False)
-        regroup(pair_a)
-        row_sums = {pair: keep.tile([P, 2], F32, name="row_sums%d" % pair) for pair in (pair_c, pair_d)}
-        for i in last:
-            tanh(i)
-            mish(i, row_sum=row_sums[i // 2][:, i % 2 : i % 2 + 1])
-            if i == last[0]:
-                second_product(pair_a)
-        statistics_on_scalar(pair_c, row_sums[pair_c])
-        scale_pair(pair_b, 0, on_scalar=False)
-        statistics_on_scalar(pair_d, row_sums[pair_d])
-        scale_pair(pair_b, 1, on_scalar=True)
-        for i in tiles_of(pair_c):
-            normalise(i)
-            flip_hidden(i)
-        corrector(pair_a)
-        for i in tiles_of(pair_d):
-            normalise(i)
-            flip_hidden(i)
-        regroup(pair_b)
-        second_product(pair_b)
-        for pair in (pair_c, pair_d):
-            for c in range(PASSES):
-                scale_pair(pair, c, on_scalar=True)
-            regroup(pair)
-            corrector(pair - 1)
-            second_product(pair)
-        corrector(pair_d)
+        regroup(0, 0)
+        regroup(0, 1)
+        scale_pass(1, 0, False)
+        quantise(0, 0)
+        quantise(0, 1)
+        second_product(0)
+        make_start_state()
+        tanh(4)
+        mish(4, True)
+        tanh(5)
+        mish(5, True)
+        tanh(6)
+        mish(6, True)
+        tanh(7)
+        square(4)
+        square(5)
+        inverse_std_after_scalar(2)
+        mish(7, True)
+        scale_pass(1, 1, False)
+        square(6)
+        square(7)
+        inverse_std_after_scalar(3)
+        copy_start_state()
+        regroup(1, 0)
+        regroup(1, 1)
+        normalise(4)
+        flip_hidden(4)
+        normalise(5)
+        flip_hidden(5)
+        corrector(0)
+        quantise(1, 0)
+        quantise(1, 1)
+        second_product(1)
+        scale_pass(2, 0, True)
+        scale_pass(2, 1, True)
+        normalise(6)
+        flip_hidden(6)
+        normalise(7)
+        flip_hidden(7)
+        corrector(1)
+        regroup(2, 0)
+        regroup(2, 1)
+        scale_pass(3, 0, True)
+        quantise(2, 0)
+        quantise(2, 1)
+        second_product(2)
+        scale_pass(3, 1, True)
+        regroup(3, 0)
+        corrector(2)
+        regroup(3, 1)
+        quantise(3, 0)
+        quantise(3, 1)
+        second_product(3)
+        corrector(3)

@@ -97,9 +97,9 @@ def tile_actorflowode_pb_kernel(tc, h0, z, k1, W1, b1, ln1_g, ln1_b, W2, b2, out
         load_w1(0, 0)
         load_w1(0, 1)
         load_h0(0)
-        load_h0(1)
         load_w1(1, 0)
         load_w1(1, 1)
+        load_h0(1)
         load_h0(2)
         load_h0(3)
         for i in range(4, TILES):
@@ -412,37 +412,37 @@ def tile_actorflowode_pb_kernel(tc, h0, z, k1, W1, b1, ln1_g, ln1_b, W2, b2, out
         vcopy, scopy = nc.vector.tensor_copy, nc.scalar.copy
         regroup_w1(0, 0, vcopy)
         transpose_h0(0, scopy)
-        transpose_h0(1, scopy)
-        spread_b1(0)
-        spread_b1(1)
         regroup_w1(0, 1, vcopy)
         quantise_w1(0, 0)
-        quantise_h0(0)
         quantise_w1(0, 1)
-        quantise_h0(1)
+        quantise_h0(0)
         regroup_w1(1, 0, scopy)
+        spread_b1(0)
         regroup_w1(1, 1, vcopy)
         multiply(0, 0)
-        multiply(1, 0)
-        transpose_h0(2, scopy)
-        transpose_h0(3, scopy)
-        add_bias(0, 0)
-        add_bias(1, 0)
+        transpose_h0(1, scopy)
+        spread_b1(1)
         quantise_w1(1, 1)
         quantise_w1(1, 0)
+        add_bias(0, 0)
+        transpose_h0(2, scopy)
+        transpose_h0(3, scopy)
+        quantise_h0(1)
         multiply(0, 1)
+        multiply(1, 0)
         multiply(1, 1)
-        quantise_h0(2)
         add_bias(0, 1)
+        sigmoid(0)
+        quantise_h0(2)
+        add_bias(1, 0)
+        add_bias(1, 1)
         multiply(2, 0)
         multiply(2, 1)
-        sigmoid(0)
+        sigmoid(1)
         quantise_h0(3)
-        add_bias(1, 1)
+        add_bias(2, 0)
         multiply(3, 0)
         multiply(3, 1)
-        sigmoid(1)
-        add_bias(2, 0)
         add_bias(2, 1)
         sigmoid(2)
         add_bias(3, 0)
@@ -457,16 +457,16 @@ def tile_actorflowode_pb_kernel(tc, h0, z, k1, W1, b1, ln1_g, ln1_b, W2, b2, out
         multiply(4, 0)
         multiply(4, 1)
         quantise_h0(6)
+        regroup_w2(vcopy)
+        quantise_h0(7)
         multiply(5, 0)
         multiply(5, 1)
         add_bias(4, 0)
-        quantise_h0(7)
         add_bias(4, 1)
         multiply(6, 0)
         multiply(6, 1)
         multiply(7, 0)
         multiply(7, 1)
-        regroup_w2(vcopy)
         add_bias(5, 0)
         add_bias(5, 1)
         quantise_w2()
@@ -483,24 +483,25 @@ def tile_actorflowode_pb_kernel(tc, h0, z, k1, W1, b1, ln1_g, ln1_b, W2, b2, out
 
         mish(0, False)
         mish(1, False)
-        partial_moments(0)
         mish(2, False)
+        partial_moments(0)
         partial_moments(1)
         join_moments(0)
         mish(3, False)
         join_moments(1)
-        partial_moments(2)
         inverse_std_after_vector(0)
-        partial_moments(3)
-        join_moments(2)
+        partial_moments(2)
         normalise(0)
         flip_hidden(0)
-        join_moments(3)
         normalise(1)
         flip_hidden(1)
+        join_moments(2)
+        partial_moments(3)
+        join_moments(3)
+        scale_block(0, 0, False)
         inverse_std_after_vector(1)
-        scale_pass(0, 0, False)
-        scale_pass(0, 1, False)
+        for j in range(1, 8):
+            scale_block(0, j, False)
         normalise(2)
         flip_hidden(2)
         normalise(3)
@@ -551,7 +552,10 @@ def tile_actorflowode_pb_kernel(tc, h0, z, k1, W1, b1, ln1_g, ln1_b, W2, b2, out
         quantise(2, 0)
         quantise(2, 1)
         second_product(2)
-        scale_pass(3, 1, True)
+        scale_block(3, 4, True)
+        scale_block(3, 5, True)
+        scale_block(3, 6, False)
+        scale_block(3, 7, False)
         regroup(3, 0)
         corrector(2)
         regroup(3, 1)

from contextlib import ExitStack

import concourse.mybir as mybir
from concourse.masks import make_identity

F32 = mybir.dt.float32
BF16 = mybir.dt.bfloat16
U32 = mybir.dt.uint32
U8 = mybir.dt.uint8
FP8X4 = mybir.dt.float8_e4m3fn_x4
FUNC = mybir.ActivationFunctionType
ALU = mybir.AluOpType

P = 128
PACK = 4
K_PASS = P * PACK
BATCH, UNITS, ACTIONS = 1024, 1024, 128
TILES = BATCH // P
BATCHES = ((0, 1, 2, 3), (4, 5, 6, 7))
GROUPS = ((0, 1), (2, 3), (4, 5), (6, 7))
PASSES = UNITS // K_PASS
BANK = 512
HALVES = UNITS // BANK
BLOCKS = UNITS // P
LN_EPS = 1e-5
QUARTER = 0.25
SMALLEST = 2.0 ** -60

FLOPS = 2 * BATCH * UNITS * UNITS + 2 * BATCH * UNITS * ACTIONS


def tile_actorflowode_pb_kernel(tc, h0, z, k1, W1, b1, ln1_g, ln1_b, W2, b2, out):
    nc = tc.nc
    with ExitStack() as ctx:
        keep = ctx.enter_context(tc.tile_pool(name="keep", bufs=1))
        psum = ctx.enter_context(tc.psum_pool(name="psum", bufs=7))
        psum_head = ctx.enter_context(tc.psum_pool(name="psum_head", bufs=1))
        ctx.enter_context(tc.manual_schedule())

        smallest = keep.tile([P, 1], F32)
        nc.vector.memset(smallest[:], SMALLEST)
        ones = keep.tile([P, P], BF16)
        nc.vector.memset(ones[:], 1.0)
        bias_rows = keep.tile([P, UNITS], BF16)
        nc.vector.memset(bias_rows[:], 0.0)
        b2_rows = keep.tile([P, PACK, ACTIONS], BF16)
        nc.vector.memset(b2_rows[:], 0.0)
        norm_split = keep.tile([P, PACK, P], BF16)
        nc.vector.memset(norm_split[:], 0.0)
        neg_half = keep.tile([P, 2], F32)
        nc.vector.memset(neg_half[:], -0.5)
        eps = keep.tile([P, 1], F32)
        nc.vector.memset(eps[:], LN_EPS)
        ident_f32 = keep.tile([P, P], F32)
        make_identity(nc, ident_f32[:])

        b1_row = keep.tile([1, UNITS], BF16)
        nc.scalar.dma_start(out=b1_row[:], in_=b1.rearrange("(o n) -> o n", o=1))
        norm_rows = keep.tile([2 * PASSES, K_PASS], BF16)
        nc.scalar.dma_start(out=norm_rows[0:PASSES, :], in_=ln1_g.rearrange("(c n) -> c n", n=K_PASS))
        nc.scalar.dma_start(
            out=norm_rows[PASSES : 2 * PASSES, :], in_=ln1_b.rearrange("(c n) -> c n", n=K_PASS)
        )
        b2_row = keep.tile([1, ACTIONS], BF16)
        nc.scalar.dma_start(out=b2_row[:], in_=b2.rearrange("(o n) -> o n", o=1))
        warm = keep.tile([P, 1], F32)
        nc.scalar.activation(out=warm[:], in_=smallest[:], func=FUNC.Sigmoid)
        ident_bf16 = keep.tile([P, P], BF16)
        nc.scalar.copy(out=ident_bf16[:], in_=ident_f32[:])
        four_bf16 = keep.tile([P, P], BF16)
        nc.scalar.mul(out=four_bf16[:], in_=ident_f32[:], mul=4.0)
        nc.scalar.copy(out=bias_rows[0:1, :], in_=b1_row[:])
        nc.scalar.copy(
            out=norm_split[0 : 2 * PASSES, :, :], in_=norm_rows[:].rearrange("r (m t) -> r t m", t=PACK)
        )
        nc.scalar.copy(out=b2_rows[0:1, :, :], in_=b2_row[:].unsqueeze(1).to_broadcast([1, PACK, ACTIONS]))

        w1_raw = {}

        def load_w1(half, g):
            cols = slice(BANK * half, BANK * (half + 1))
            raw = keep.tile([P, PACK, BANK], BF16, name="w1_raw%d%d" % (half, g))
            nc.sync.dma_start(
                out=raw[:], in_=W1[K_PASS * g : K_PASS * (g + 1), cols].rearrange("(p t) n -> p t n", t=PACK)
            )
            w1_raw[(half, g)] = raw

        h0_raw = {}

        def load_h0(i):
            h0_raw[i] = keep.tile([P, UNITS], BF16, name="h0_raw%d" % i)
            nc.sync.dma_start(out=h0_raw[i][:], in_=h0[P * i : P * (i + 1), :])

        z_rows = keep.tile([P, TILES, ACTIONS], BF16)
        k1_rows = keep.tile([P, TILES, ACTIONS], BF16)
        w2_raw = keep.tile([P, PASSES, PACK, ACTIONS], BF16)
        load_w1(0, 0)
        load_w1(0, 1)
        load_h0(0)
        load_w1(1, 0)
        load_w1(1, 1)
        load_h0(1)
        load_h0(2)
        load_h0(3)
        for i in range(4, TILES):
            load_h0(i)
        nc.sync.dma_start(out=w2_raw[:], in_=W2.rearrange("(c p t) a -> p c t a", p=P, t=PACK))
        nc.sync.dma_start(out=z_rows[:], in_=z.rearrange("(i p) a -> p i a", p=P))
        nc.sync.dma_start(out=k1_rows[:], in_=k1.rearrange("(i p) a -> p i a", p=P))

        bias1 = keep.tile([P, UNITS], BF16)

        def spread_b1(half):
            cols = slice(BANK * half, BANK * (half + 1))
            spread = psum.tile([P, BANK], F32, tag="bank", name="spread")
            nc.tensor.matmul(out=spread[:], lhsT=ones[:], rhs=bias_rows[:, cols], start=True, stop=True)
            nc.scalar.copy(
                out=bias1[:, cols].rearrange("p (t m) -> p t m", t=PACK),
                in_=spread[:].rearrange("p (m t) -> p t m", t=PACK),
            )

        small = {}
        gain = keep.tile([P, BLOCKS], F32)
        shift = keep.tile([P, BLOCKS], F32)

        def norm_columns():
            norm_cols = psum.tile([P, PACK, P], BF16, tag="bank", name="norm_cols")
            for t in range(PACK):
                nc.tensor.transpose(norm_cols[:, t, :], norm_split[:, t, :], ident_bf16[:])
            small["norm_cols"] = norm_cols

        def copy_norm_columns():
            norm_cols = small["norm_cols"]
            nc.scalar.copy(
                out=gain[:].rearrange("p (c t) -> p c t", t=PACK),
                in_=norm_cols[:, :, 0:PASSES].rearrange("p t c -> p c t"),
            )
            nc.scalar.copy(
                out=shift[:].rearrange("p (c t) -> p c t", t=PACK),
                in_=norm_cols[:, :, PASSES : 2 * PASSES].rearrange("p t c -> p c t"),
            )

        start_state = keep.tile([P, TILES, ACTIONS], F32)

        def make_start_state():
            for n in range(2):
                tiles = slice(PACK * n, PACK * (n + 1))
                total = psum.tile([P, PACK, ACTIONS], F32, tag="bank", name="total")
                terms = ((four_bf16, z_rows[:, tiles, :]), (ident_bf16, k1_rows[:, tiles, :]), (ones, b2_rows[:]))
                for k, (left, right) in enumerate(terms):
                    nc.tensor.matmul(
                        out=total[:].rearrange("p i a -> p (i a)"), lhsT=left[:],
                        rhs=right.rearrange("p i a -> p (i a)"), start=(k == 0), stop=(k == 2),
                    )
                small[n] = total

        def copy_start_state():
            for n in range(2):
                tiles = slice(PACK * n, PACK * (n + 1))
                nc.scalar.activation(out=start_state[:, tiles, :], in_=small[n][:], func=FUNC.Copy, scale=QUARTER)

        w1_codes = {}
        w1_scales = {}
        w1_grouped = {}
        for half in range(HALVES):
            for g in range(PASSES):
                w1_codes[(half, g)] = keep.tile([P, BANK], U32, align_bytes=64, name="w1_codes%d%d" % (half, g))
                w1_scales[(half, g)] = keep.tile([P, BANK], U8, align_bytes=64, name="w1_scales%d%d" % (half, g))

        def regroup_w1(half, g, copy):
            grouped = keep.tile([P, BANK, PACK], BF16, align_bytes=64, name="w1_grouped%d%d" % (half, g))
            copy(
                out=grouped[:].rearrange("p (c i) t -> p c t i", i=4),
                in_=w1_raw[(half, g)][:].rearrange("p t (c i) -> p c t i", i=4),
            )
            w1_grouped[(half, g)] = grouped

        def quantise_w1(half, g):
            nc.vector.quantize_mx(
                out=w1_codes[(half, g)][:].bitcast(FP8X4), scales=w1_scales[(half, g)][:],
                in_=w1_grouped[(half, g)][:].rearrange("p n t -> p (n t)"),
            )

        h0_codes = keep.tile([P, TILES, PASSES * P], U32, align_bytes=64)
        h0_scales = keep.tile([P, TILES, PASSES * P], U8, align_bytes=64)
        h0_grouped = {}
        pre_batch, work_batch, pre, work = {}, {}, {}, {}
        for n, batch in enumerate(BATCHES):
            pre_batch[n] = keep.tile([P, len(batch), UNITS], F32, name="pre_batch%d" % n)
            work_batch[n] = keep.tile([P, len(batch), UNITS], F32, name="work_batch%d" % n)
            for k, i in enumerate(batch):
                pre[i] = pre_batch[n][:, k, :]
                work[i] = work_batch[n][:, k, :]
        group_of = {i: (q, k) for q, group in enumerate(GROUPS) for k, i in enumerate(group)}

        def transpose_h0(i, copy):
            words = h0_raw[i][:].bitcast(F32)
            turned = psum.tile([P, PACK, P], F32, tag="bank", name="turned")
            for g in range(PASSES):
                for u in range(2):
                    nc.tensor.transpose(
                        turned[:, 2 * g + u, :], words[:, 2 * P * g + u : 2 * P * (g + 1) : 2], ident_f32[:]
                    )
            h0_grouped[i] = keep.tile([P, UNITS], BF16, align_bytes=64, name="h0_grouped%d" % i)
            copy(
                out=h0_grouped[i][:].bitcast(F32).rearrange("p (g b u) -> p g b u", g=PASSES, u=2),
                in_=turned[:].rearrange("p (g u) b -> p g b u", u=2),
            )

        def quantise_h0(i):
            nc.vector.quantize_mx(
                out=h0_codes[:, i, :].bitcast(FP8X4), scales=h0_scales[:, i, :], in_=h0_grouped[i][:]
            )

        acc = {}

        def multiply(i, half):
            acc[(i, half)] = psum.tile([P, BANK], F32, tag="bank", name="acc")
            for g in range(PASSES):
                rows = slice(P * g, P * (g + 1))
                nc.tensor.matmul_mx(
                    out=acc[(i, half)][:],
                    lhsT=h0_codes[:, i, rows].bitcast(FP8X4), lhsT_scale=h0_scales[:, i, rows],
                    rhs=w1_codes[(half, g)][:].bitcast(FP8X4), rhs_scale=w1_scales[(half, g)][:],
                    start=(g == 0), stop=(g == PASSES - 1),
                )

        def add_bias(i, half):
            cols = slice(BANK * half, BANK * (half + 1))
            nc.vector.tensor_tensor(
                out=pre[i][:, cols].rearrange("p (t m) -> p t m", t=PACK),
                in0=acc[(i, half)][:].rearrange("p (m t) -> p t m", t=PACK),
                in1=bias1[:, cols].rearrange("p (t m) -> p t m", t=PACK),
                op=ALU.add,
            )

        def sigmoid(i):
            nc.scalar.activation(out=work[i], in_=pre[i], func=FUNC.Sigmoid, scale=-1.0)

        def sigmoid_batch(n):
            nc.scalar.activation(out=work_batch[n][:], in_=pre_batch[n][:], func=FUNC.Sigmoid, scale=-1.0)

        def log(n):
            nc.scalar.activation(out=work_batch[n][:], in_=work_batch[n][:], func=FUNC.Ln, bias=smallest[:])

        def tanh(i):
            nc.scalar.activation(out=work[i], in_=work[i], func=FUNC.Tanh, scale=-1.0)

        row_sums = {}

        def mish(i, with_sum):
            q, k = group_of[i]
            if with_sum and k == 0:
                row_sums[q] = keep.tile([P, len(GROUPS[q])], F32, name="row_sums%d" % q)
            nc.vector.scalar_tensor_tensor(
                out=pre[i], in0=pre[i], scalar=1.0, in1=work[i], op0=ALU.mult, op1=ALU.mult,
                accum_out=row_sums[q][:, k : k + 1] if with_sum else None,
            )

        mean = {}
        inv_std = {}
        moments = {}
        parts = {}
        squares = {}

        def inverse_std(q, padded):
            width = len(GROUPS[q])
            result = keep.tile([P, width], F32, name="inv_std%d" % q)
            nc.gpsimd.tensor_tensor(out=result[:], in0=padded[:], in1=neg_half[:, 0:width], op=ALU.pow)
            for k, i in enumerate(GROUPS[q]):
                inv_std[i] = result[:, k : k + 1]

        def partial_moments(i):
            parts[i] = keep.tile([P, HALVES, 6], F32, name="parts%d" % i)
            for half in range(HALVES):
                nc.vector.bn_stats(out=parts[i][:, half, :], in_=pre[i][:, BANK * half : BANK * (half + 1)])

        def join_moments(i):
            q, k = group_of[i]
            if k == 0:
                moments[q] = keep.tile([P, len(GROUPS[q]), 2], F32, name="moments%d" % q)
            nc.vector.bn_aggr(out=moments[q][:, k, :], in_=parts[i][:].rearrange("p h s -> p (h s)"))
            mean[i] = moments[q][:, k, 0:1]

        def inverse_std_after_vector(q):
            padded = keep.tile([P, len(GROUPS[q])], F32, name="padded%d" % q)
            nc.vector.tensor_scalar_add(out=padded[:], in0=moments[q][:, :, 1], scalar1=LN_EPS)
            inverse_std(q, padded)

        def square(i):
            q, k = group_of[i]
            if k == 0:
                squares[q] = keep.tile([P, len(GROUPS[q])], F32, name="squares%d" % q)
            nc.scalar.activation(
                out=work[i], in_=pre[i], func=FUNC.Square, bias=row_sums[q][:, k : k + 1],
                scale=-1.0 * UNITS, accum_out=squares[q][:, k : k + 1],
            )

        def inverse_std_after_scalar(q):
            means = keep.tile([P, len(GROUPS[q])], F32, name="means%d" % q)
            nc.scalar.mul(out=means[:], in_=row_sums[q][:], mul=1.0 / UNITS)
            for k, i in enumerate(GROUPS[q]):
                mean[i] = means[:, k : k + 1]
            padded = keep.tile([P, len(GROUPS[q])], F32, name="padded%d" % q)
            nc.scalar.activation(
                out=padded[:], in_=squares[q][:], func=FUNC.Identity, bias=eps[:], scale=1.0 / UNITS ** 3
            )
            inverse_std(q, padded)

        def normalise(i):
            nc.vector.tensor_scalar(
                out=work[i], in0=pre[i], scalar1=mean[i], scalar2=inv_std[i], op0=ALU.subtract, op1=ALU.mult
            )

        flipped = {}

        def flip_hidden(i):
            q, k = group_of[i]
            width = P * len(GROUPS[q])
            each = BANK // width
            if k == 0:
                flipped[q] = []
                for n in range(BLOCKS // each):
                    bank = psum.tile([P, each, width], F32, tag="bank", name="flipped%d" % n)
                    flipped[q] += [bank[:, b, :] for b in range(each)]
            for j in range(BLOCKS):
                nc.tensor.transpose(
                    flipped[q][j][:, P * k : P * (k + 1)], work[i][:, P * j : P * (j + 1)], ident_f32[:]
                )

        planes = {}

        def scale_block(q, j, on_scalar):
            if q not in planes:
                planes[q] = keep.tile([P, BLOCKS, P * len(GROUPS[q])], BF16, name="planes%d" % q)
            if on_scalar:
                nc.scalar.activation(
                    out=planes[q][:, j, :], in_=flipped[q][j], func=FUNC.Identity,
                    bias=shift[:, j : j + 1], scale=gain[:, j : j + 1],
                )
            else:
                nc.vector.tensor_scalar(
                    out=planes[q][:, j, :], in0=flipped[q][j],
                    scalar1=gain[:, j : j + 1], scalar2=shift[:, j : j + 1], op0=ALU.mult, op1=ALU.add,
                )

        def scale_pass(q, c, on_scalar):
            for j in range(PACK * c, PACK * (c + 1)):
                scale_block(q, j, on_scalar)

        w2_codes = keep.tile([P, PASSES * ACTIONS], U32, align_bytes=64)
        w2_scales = keep.tile([P, PASSES * ACTIONS], U8, align_bytes=64)
        w2_grouped = keep.tile([P, PASSES, ACTIONS, PACK], BF16, align_bytes=64)

        def regroup_w2(copy):
            copy(out=w2_grouped[:], in_=w2_raw[:].rearrange("p c t a -> p c a t"))

        def quantise_w2():
            nc.vector.quantize_mx(
                out=w2_codes[:].bitcast(FP8X4), scales=w2_scales[:],
                in_=w2_grouped[:].rearrange("p c a t -> p (c a t)"),
            )

        grouped = {}
        codes = {}
        scales = {}
        head_sums = psum_head.tile([P, PACK, ACTIONS], F32, name="head_sums")

        def regroup(q, c):
            rows = P * len(GROUPS[q])
            if q not in grouped:
                grouped[q] = keep.tile([P, PASSES, rows, PACK], BF16, align_bytes=64, name="h1_grouped%d" % q)
                codes[q] = keep.tile([P, PASSES, rows], U32, align_bytes=64, name="h1_codes%d" % q)
                scales[q] = keep.tile([P, PASSES, rows], U8, align_bytes=64, name="h1_scales%d" % q)
            nc.vector.tensor_copy(
                out=grouped[q][:, c, :, :].rearrange("p (c i) t -> p c t i", i=4),
                in_=planes[q][:, PACK * c : PACK * (c + 1), :].rearrange("p t (c i) -> p c t i", i=4),
            )

        def quantise(q, c):
            nc.vector.quantize_mx(
                out=codes[q][:, c, :].bitcast(FP8X4), scales=scales[q][:, c, :],
                in_=grouped[q][:, c, :, :].rearrange("p b t -> p (b t)"),
            )

        def second_product(q):
            for k in range(len(GROUPS[q])):
                rows = slice(P * k, P * (k + 1))
                for c in range(PASSES):
                    cols = slice(ACTIONS * c, ACTIONS * (c + 1))
                    nc.tensor.matmul_mx(
                        out=head_sums[:, 2 * (q % 2) + k, :],
                        lhsT=codes[q][:, c, rows].bitcast(FP8X4), lhsT_scale=scales[q][:, c, rows],
                        rhs=w2_codes[:, cols].bitcast(FP8X4), rhs_scale=w2_scales[:, cols],
                        start=(c == 0), stop=(c == PASSES - 1),
                    )

        def corrector(q):
            first, width = GROUPS[q][0], len(GROUPS[q])
            slot = 2 * (q % 2)
            result = keep.tile([P, width, ACTIONS], F32, name="result%d" % q)
            nc.vector.scalar_tensor_tensor(
                out=result[:], in0=head_sums[:, slot : slot + width, :], scalar=QUARTER,
                in1=start_state[:, first : first + width, :], op0=ALU.mult, op1=ALU.add,
            )
            nc.sync.dma_start(
                out=out[P * first : P * (first + width), :].rearrange("(r p) a -> p r a", p=P),
                in_=result[:],
            )


        vcopy, scopy = nc.vector.tensor_copy, nc.scalar.copy
        regroup_w1(0, 0, vcopy)
        transpose_h0(0, scopy)
        regroup_w1(0, 1, vcopy)
        quantise_w1(0, 0)
        quantise_w1(0, 1)
        quantise_h0(0)
        regroup_w1(1, 0, scopy)
        spread_b1(0)
        regroup_w1(1, 1, vcopy)
        multiply(0, 0)
        transpose_h0(1, scopy)
        spread_b1(1)
        quantise_w1(1, 1)
        quantise_w1(1, 0)
        add_bias(0, 0)
        transpose_h0(2, scopy)
        transpose_h0(3, scopy)
        quantise_h0(1)
        multiply(0, 1)
        multiply(1, 0)
        multiply(1, 1)
        add_bias(0, 1)
        sigmoid(0)
        quantise_h0(2)
        add_bias(1, 0)
        add_bias(1, 1)
        multiply(2, 0)
        multiply(2, 1)
        sigmoid(1)
        quantise_h0(3)
        add_bias(2, 0)
        multiply(3, 0)
        multiply(3, 1)
        add_bias(2, 1)
        sigmoid(2)
        add_bias(3, 0)
        add_bias(3, 1)
        sigmoid(3)
        log(0)
        nc.scalar.activation(out=warm[:], in_=smallest[:], func=FUNC.Sigmoid)
        for i in (4, 5, 6, 7):
            transpose_h0(i, vcopy)
        quantise_h0(4)
        quantise_h0(5)
        multiply(4, 0)
        multiply(4, 1)
        quantise_h0(6)
        regroup_w2(vcopy)
        quantise_h0(7)
        multiply(5, 0)
        multiply(5, 1)
        add_bias(4, 0)
        add_bias(4, 1)
        multiply(6, 0)
        multiply(6, 1)
        multiply(7, 0)
        multiply(7, 1)
        add_bias(5, 0)
        add_bias(5, 1)
        quantise_w2()
        add_bias(6, 0)
        add_bias(6, 1)
        add_bias(7, 0)
        add_bias(7, 1)
        norm_columns()
        for i in range(4):
            tanh(i)
        copy_norm_columns()
        sigmoid_batch(1)
        log(1)

        mish(0, False)
        mish(1, False)
        mish(2, False)
        partial_moments(0)
        partial_moments(1)
        join_moments(0)
        mish(3, False)
        join_moments(1)
        inverse_std_after_vector(0)
        partial_moments(2)
        normalise(0)
        flip_hidden(0)
        normalise(1)
        flip_hidden(1)
        join_moments(2)
        partial_moments(3)
        join_moments(3)
        scale_block(0, 0, False)
        inverse_std_after_vector(1)
        for j in range(1, 8):
            scale_block(0, j, False)
        normalise(2)
        flip_hidden(2)
        normalise(3)
        flip_hidden(3)
        regroup(0, 0)
        regroup(0, 1)
        scale_pass(1, 0, False)
        quantise(0, 0)
        quantise(0, 1)
        second_product(0)
        make_start_state()
        tanh(4)
        mish(4, True)
        tanh(5)
        mish(5, True)
        tanh(6)
        mish(6, True)
        tanh(7)
        square(4)
        square(5)
        inverse_std_after_scalar(2)
        mish(7, True)
        scale_pass(1, 1, False)
        square(6)
        square(7)
        inverse_std_after_scalar(3)
        copy_start_state()
        regroup(1, 0)
        regroup(1, 1)
        normalise(4)
        flip_hidden(4)
        normalise(5)
        flip_hidden(5)
        corrector(0)
        quantise(1, 0)
        quantise(1, 1)
        second_product(1)
        scale_pass(2, 0, True)
        scale_pass(2, 1, True)
        normalise(6)
        flip_hidden(6)
        normalise(7)
        flip_hidden(7)
        corrector(1)
        regroup(2, 0)
        regroup(2, 1)
        scale_pass(3, 0, True)
        quantise(2, 0)
        quantise(2, 1)
        second_product(2)
        scale_block(3, 4, True)
        scale_block(3, 5, True)
        scale_block(3, 6, False)
        scale_block(3, 7, False)
        regroup(3, 0)
        corrector(2)
        regroup(3, 1)
        quantise(3, 0)
        quantise(3, 1)
        second_product(3)
        corrector(3)
